import numpy as np
import ml_dtypes


def mxq(x, axis, fmt="e4m3"):
    dtype, down = {"e4m3": (ml_dtypes.float8_e4m3fn, 7), "e5m2": (ml_dtypes.float8_e5m2, 14)}[fmt]
    v = np.moveaxis(np.asarray(x, np.float32).astype(ml_dtypes.bfloat16).astype(np.float64), axis, -1)
    blocks = v.reshape(v.shape[:-1] + (-1, 32))
    amax = np.abs(blocks).max(-1, keepdims=True)
    byte = np.maximum(np.where(amax > 0, np.frexp(amax)[1] - 1 + 127, 0) - down, 1)
    scale = np.exp2(byte - 127.0)
    codes = (blocks / scale).astype(np.float32).astype(dtype).astype(np.float64)
    return np.moveaxis((codes * scale).reshape(v.shape), -1, axis)


WIDE = False


def mx_kscale(k):
    if not WIDE:
        return np.ones(k)
    levels = np.array([10, -10, 5, -5, 0])
    if k % 512:
        return np.exp2(np.random.permutation(np.resize(levels, k // 32))).repeat(32)
    a = np.empty((k // 512, 16))
    for p in range(k // 512):
        a[p, :8] = np.random.permutation(np.resize(levels, 8))
        for g in range(8):
            far = levels[np.abs(levels - a[p, g]) >= 10]
            a[p, g + 8] = far[np.random.randint(len(far))]
    return np.exp2(a.ravel()).repeat(32)


BF16 = ml_dtypes.bfloat16


def bf(x):
    return np.asarray(x, np.float32).astype(BF16)


def f64(x):
    return np.asarray(x).astype(np.float64)


H, D_CONTENT, D_POS, D_K, D_V, B, L = 8, 768, 256, 128, 128, 4, 256
D_MODEL = D_CONTENT + D_POS
T = B * L
DV1 = D_V // 2
KP = H * DV1
EPS = 1e-3


def setup_inputs():
    s1, s2 = mx_kscale(KP), mx_kscale(KP)
    sc = np.concatenate([s1.reshape(H, DV1), s2.reshape(H, DV1)], axis=1)
    return {
        "attn_out": bf(np.random.standard_normal((H, B, L, D_V)) * 0.4 * sc[:, None, None, :]),
        "inp": bf(np.random.standard_normal((T, D_MODEL)) * 0.05 + np.random.standard_normal((T, 1)) * 0.03),
        "w_proj1": bf(np.random.standard_normal((KP, D_CONTENT)) * 0.1 / np.sqrt(KP) / s1[:, None]),
        "w_proj2": bf(np.random.standard_normal((KP, D_POS)) * 0.1 / np.sqrt(KP) / s2[:, None]),
        "ln_a": bf(1.0 + 0.1 * np.random.standard_normal(D_MODEL)),
        "ln_b": bf(0.1 * np.random.standard_normal(D_MODEL)),
    }


def core(attn_out, inp, w_proj1, w_proj2, ln_a, ln_b):
    o = f64(attn_out).reshape(H, T, D_V).transpose(1, 0, 2)
    o1 = o[:, :, :DV1].reshape(T, KP)
    o2 = o[:, :, DV1:].reshape(T, KP)
    y1 = mxq(o1, 1, "e4m3") @ mxq(f64(w_proj1), 0, "e4m3")
    y2 = mxq(o2, 1, "e4m3") @ mxq(f64(w_proj2), 0, "e4m3")
    z = np.concatenate([y1, y2], -1) + f64(inp)
    mu = np.mean(z, axis=-1, keepdims=True)
    sigma = np.std(z, axis=-1, keepdims=True, ddof=1)
    ln = (z - mu) / (sigma + EPS)
    return ln * f64(ln_a) + f64(ln_b)


def e4m3fn_bytes(y):
    return np.clip(np.asarray(y, np.float64), -448.0, 448.0).astype(np.float32).astype(ml_dtypes.float8_e4m3fn).view(np.uint8)


Y_SCALE = 220.0


def reference(attn_out, inp, w_proj1, w_proj2, ln_a, ln_b):
    out = core(attn_out, inp, w_proj1, w_proj2, ln_a, ln_b)
    return out, e4m3fn_bytes(out * Y_SCALE)

@@ -1,0 +1,322 @@
+from contextlib import ExitStack
+
+import concourse.mybir as mybir
+from concourse.masks import make_identity
+
+F32 = mybir.dt.float32
+BF16 = mybir.dt.bfloat16
+U32 = mybir.dt.uint32
+U8 = mybir.dt.uint8
+FP8X4 = mybir.dt.float8_e4m3fn_x4
+FP8 = mybir.dt.float8_e4m3fn
+ALU = mybir.AluOpType
+ACT = mybir.ActivationFunctionType
+
+P = 128
+H = 8
+N = 1024
+NT = 8
+EPS = 1e-3
+Y_SCALE = 220.0
+CW = 320
+C0 = N - CW
+
+FLOPS = 2 * 1024 * 512 * 1024
+
+
+def tile_multiheadattention_pa_kernel(tc, attn_out, inp, w_proj1, w_proj2, ln_a, ln_b, out_0, out_1):
+    nc = tc.nc
+    attn = attn_out.rearrange("h b l f -> h (b l) f")
+
+    with ExitStack() as ctx:
+        keep = ctx.enter_context(tc.tile_pool(name="keep", bufs=1))
+        loads = ctx.enter_context(tc.tile_pool(name="loads", bufs=4))
+        work = ctx.enter_context(tc.tile_pool(name="work", bufs=3))
+        stats = ctx.enter_context(tc.tile_pool(name="stats", bufs=4))
+        ps_const = ctx.enter_context(tc.psum_pool(name="ps_const", bufs=1))
+        ps_t = ctx.enter_context(tc.psum_pool(name="ps_t", bufs=2))
+        ps_acc = ctx.enter_context(tc.psum_pool(name="ps_acc", bufs=2))
+        ctx.enter_context(tc.manual_schedule())
+
+        warm = keep.tile([P, 1], F32, name="warm")
+        warm2 = keep.tile([P, 1], F32, name="warm2")
+        ab_row = keep.tile([P, 2 * N], BF16, name="ab_row")
+        ones = keep.tile([P, P], BF16, name="ones")
+        ident = keep.tile([P, P], F32, name="ident")
+        nc.vector.memset(warm[:], 1.0)
+        nc.vector.memset(ab_row[:], 0.0)
+        nc.vector.memset(ones[:], 1.0)
+        nc.scalar.activation(out=warm2[:], in_=warm[:], func=ACT.Sqrt)
+        make_identity(nc, ident[:])
+
+        x_raw = {}
+        inp_sb = {}
+        w_raw = {}
+
+        def load_x(c):
+            t = loads.tile([P, H, 256], BF16, name="x_raw")
+            nc.sync.dma_start(out=t[:], in_=attn[:, 256 * c : 256 * (c + 1), :].rearrange("h (p i) f -> p h (i f)", i=2))
+            x_raw[c] = t
+
+        def load_inp(c):
+            t = loads.tile([P, 2 * N], BF16, name="inp_sb")
+            nc.sync.dma_start(out=t[:], in_=inp[256 * c : 256 * (c + 1), :].rearrange("(p i) n -> p (i n)", i=2))
+            inp_sb[c] = t
+
+        def load_w(c):
+            t = loads.tile([P, 4, 256], BF16, name="w_raw")
+            src = w_proj1[:, 256 * c : 256 * (c + 1)] if c < 3 else w_proj2
+            nc.sync.dma_start(out=t[:], in_=src.rearrange("(p j) w -> p j w", j=4))
+            w_raw[c] = t
+
+        load_x(0)
+        for c in range(4):
+            load_w(c)
+        nc.sync.dma_start(out=ab_row[0:1, 0:N], in_=ln_a.rearrange("(o n) -> o n", o=1))
+        nc.sync.dma_start(out=ab_row[0:1, N : 2 * N], in_=ln_b.rearrange("(o n) -> o n", o=1))
+        load_inp(0)
+        for c in range(1, 4):
+            load_x(c)
+            load_inp(c)
+
+        a_ps = ps_const.tile([P, N], BF16, name="a_ps")
+        b_ps = ps_const.tile([P, N], BF16, name="b_ps")
+        a_sb = keep.tile([P, max(CW, 64)], BF16, name="a_sb")
+        b_sb = keep.tile([P, max(CW, 64)], BF16, name="b_sb")
+
+        def spread_ab():
+            for half in range(2):
+                cols = slice(512 * half, 512 * (half + 1))
+                nc.tensor.matmul(out=a_ps[:, cols], lhsT=ones[:], rhs=ab_row[:, 512 * half : 512 * (half + 1)], start=True, stop=True)
+            for half in range(2):
+                cols = slice(512 * half, 512 * (half + 1))
+                nc.tensor.matmul(out=b_ps[:, cols], lhsT=ones[:], rhs=ab_row[:, N + 512 * half : N + 512 * (half + 1)], start=True, stop=True)
+
+        def copy_ab():
+            if CW > 0:
+                nc.scalar.copy(out=a_sb[:, 0:CW], in_=a_ps[:, C0:N])
+                nc.scalar.copy(out=b_sb[:, 0:CW], in_=b_ps[:, C0:N])
+
+        w_g = keep.tile([P, 4 * N], BF16, name="w_g", align_bytes=64)
+        w_c = keep.tile([P, N], U32, name="w_c", align_bytes=64)
+        w_s = keep.tile([P, N], U8, name="w_s", align_bytes=64)
+
+        def w_interleave(eng_copy, c):
+            eng_copy(
+                out=w_g[:, 1024 * c : 1024 * (c + 1)].rearrange("p (w j) -> p w j", j=4),
+                in_=w_raw[c][:].rearrange("p j w -> p w j"),
+            )
+
+        def w_quant(c):
+            nc.vector.quantize_mx(
+                out=w_c[:, 256 * c : 256 * (c + 1)].bitcast(FP8X4),
+                scales=w_s[:, 256 * c : 256 * (c + 1)],
+                in_=w_g[:, 1024 * c : 1024 * (c + 1)],
+            )
+
+        xs_t = {}
+        xt_t = {}
+        g_t = {}
+        xc_t = {}
+        acc_t = {}
+        z_t = {}
+        sv_t = {}
+        ss_t = {}
+        t_t = {}
+        og_t = {}
+        o_t = {}
+        o8_t = {}
+
+        def share(j):
+            return CW if j < NT - 1 else 0
+
+        def out_rows(dram, j):
+            c, i = divmod(j, 2)
+            return dram[256 * c : 256 * (c + 1), :].rearrange("(p i) n -> p i n", i=2)[:, i, :]
+
+        def stage_r(j):
+            c, i = divmod(j, 2)
+            xs = work.tile([P, 1024], BF16, name="xs")
+            xw = x_raw[c][:].bitcast(F32).rearrange("p h (i f v) -> p i f h v", i=2, f=2)
+            nc.scalar.copy(out=xs[:].bitcast(F32).rearrange("p (f h v) -> p f h v", f=2, h=H), in_=xw[:, i])
+            xs_t[j] = xs
+
+        def stage_t(j):
+            xt = ps_t.tile([P, 4, P], F32, name="xt")
+            xw = xs_t[j][:].bitcast(F32)
+            for f in range(2):
+                for u in range(2):
+                    nc.tensor.transpose(xt[:, 2 * f + u, :], xw[:, 256 * f + u : 256 * (f + 1) : 2], ident[:])
+            xt_t[j] = xt
+
+        def stage_e(j):
+            g = work.tile([P, 1024], BF16, name="g", align_bytes=64)
+            nc.scalar.copy(
+                out=g[:].bitcast(F32).rearrange("p (f r u) -> p f r u", f=2, u=2),
+                in_=xt_t[j][:].rearrange("p (f u) r -> p f r u", u=2),
+            )
+            g_t[j] = g
+
+        def stage_q(j):
+            xc = work.tile([P, 256], U32, name="xc", align_bytes=64)
+            xsc = work.tile([P, 256], U8, name="xsc", align_bytes=64)
+            nc.vector.quantize_mx(out=xc[:].bitcast(FP8X4), scales=xsc[:], in_=g_t[j][:])
+            xc_t[j] = (xc, xsc)
+
+        def mm(out, xc, xsc, xcols, wcols):
+            nc.tensor.matmul_mx(
+                out=out,
+                lhsT=xc[:, xcols].bitcast(FP8X4),
+                lhsT_scale=xsc[:, xcols],
+                rhs=w_c[:, wcols].bitcast(FP8X4),
+                rhs_scale=w_s[:, wcols],
+                start=True,
+                stop=True,
+            )
+
+        def stage_m(j):
+            xc, xsc = xc_t[j]
+            acc0 = ps_acc.tile([P, 512], F32, name="acc0")
+            acc1 = ps_acc.tile([P, 512], F32, name="acc1")
+            mm(acc0[:], xc, xsc, slice(0, 128), slice(0, 512))
+            mm(acc1[:, 0:256], xc, xsc, slice(0, 128), slice(512, 768))
+            mm(acc1[:, 256:512], xc, xsc, slice(128, 256), slice(768, 1024))
+            acc_t[j] = (acc0, acc1)
+
+        def stage_ab(j, b):
+            c, i = divmod(j, 2)
+            if b == 0:
+                z_t[j] = work.tile([P, N], F32, name="z")
+                sv_t[j] = stats.tile([P, 8], F32, name="sv")
+            nc.vector.scalar_tensor_tensor(
+                out=z_t[j][:, 512 * b : 512 * (b + 1)],
+                in0=acc_t[j][b][:],
+                scalar=1.0,
+                in1=inp_sb[c][:, N * i + 512 * b : N * i + 512 * (b + 1)],
+                op0=ALU.mult,
+                op1=ALU.add,
+                accum_out=sv_t[j][:, b : b + 1],
+            )
+
+        def stage_n(j):
+            sv = sv_t[j]
+            nc.vector.tensor_scalar(
+                out=sv[:, 2:3], in0=sv[:, 0:1], scalar1=sv[:, 1:2], scalar2=-1.0 / N, op0=ALU.add, op1=ALU.mult
+            )
+
+        def stage_p2(j):
+            junk = work.tile([P, N], BF16, name="junk")
+            ss = stats.tile([P, 8], F32, name="ss")
+            nc.scalar.activation(
+                out=junk[:], in_=z_t[j][:], func=ACT.Square, bias=sv_t[j][:, 2:3], scale=1.0, accum_out=ss[:, 0:1]
+            )
+            ss_t[j] = ss
+
+        def stage_sqrt(j):
+            nc.scalar.activation(out=ss_t[j][:, 1:2], in_=ss_t[j][:, 0:1], func=ACT.Sqrt, scale=1.0 / (N - 1))
+
+        def stage_p3(j):
+            wv = N - share(j)
+            t = work.tile([P, N], F32, name="t")
+            nc.vector.scalar_tensor_tensor(
+                out=t[:, 0:wv], in0=z_t[j][:, 0:wv], scalar=sv_t[j][:, 2:3], in1=a_ps[:, 0:wv], op0=ALU.add, op1=ALU.mult
+            )
+            t_t[j] = t
+
+        def stage_eps(j):
+            nc.vector.tensor_scalar(out=sv_t[j][:, 3:4], in0=ss_t[j][:, 1:2], scalar1=EPS, scalar2=None, op0=ALU.add)
+
+        def stage_rec(j):
+            nc.vector.reciprocal(out=sv_t[j][:, 4:5], in_=sv_t[j][:, 3:4])
+
+        def stage_side(j):
+            if share(j) == 0:
+                return
+            u = work.tile([P, CW], F32, name="u")
+            nc.gpsimd.tensor_scalar(
+                out=u[:], in0=z_t[j][:, C0:N], scalar1=sv_t[j][:, 2:3], scalar2=sv_t[j][:, 4:5], op0=ALU.add, op1=ALU.mult
+            )
+            v = work.tile([P, CW], F32, name="v")
+            og = work.tile([P, CW], F32, name="og")
+            nc.gpsimd.tensor_tensor(out=v[:], in0=u[:], in1=a_sb[:, 0:CW], op=ALU.mult)
+            nc.gpsimd.tensor_tensor(out=og[:], in0=v[:], in1=b_sb[:, 0:CW], op=ALU.add)
+            og_t[j] = og
+
+        def stage_p45(j, pieces):
+            wv = N - share(j)
+            o = work.tile([P, N], F32, name="o")
+            o8 = work.tile([P, N], FP8, name="o8")
+            o8_t[j] = o8
+            w = wv // pieces
+            for k in range(pieces):
+                cols = slice(w * k, w * (k + 1))
+                nc.vector.scalar_tensor_tensor(
+                    out=o[:, cols], in0=t_t[j][:, cols], scalar=sv_t[j][:, 4:5], in1=b_ps[:, cols], op0=ALU.mult, op1=ALU.add
+                )
+                nc.sync.dma_start(out=out_rows(out_0, j)[:, cols], in_=o[:, cols])
+                if share(j) == 0:
+                    nc.scalar.activation(out=o8[:, cols], in_=o[:, cols], func=ACT.Copy, scale=Y_SCALE, saturate=False)
+                    nc.sync.dma_start(out=out_rows(out_1, j)[:, cols], in_=o8[:, cols].bitcast(U8))
+            o_t[j] = o
+
+        def stage_cast(j):
+            nc.scalar.activation(out=o8_t[j][:, 0:C0], in_=o_t[j][:, 0:C0], func=ACT.Copy, scale=Y_SCALE, saturate=False)
+
+        def stage_side_out(j):
+            if share(j) == 0:
+                return
+            nc.sync.dma_start(out=out_rows(out_0, j)[:, C0:N], in_=og_t[j][:])
+            nc.scalar.activation(out=o8_t[j][:, C0:N], in_=og_t[j][:], func=ACT.Copy, scale=Y_SCALE, saturate=False)
+            nc.sync.dma_start(out=out_rows(out_1, j), in_=o8_t[j][:].bitcast(U8))
+
+        stage_r(0)
+        stage_r(1)
+        stage_t(0)
+        stage_t(1)
+        w_interleave(nc.vector.tensor_copy, 0)
+        w_interleave(nc.vector.tensor_copy, 1)
+        stage_e(0)
+        w_interleave(nc.scalar.copy, 2)
+        w_quant(0)
+        w_quant(1)
+        w_interleave(nc.vector.tensor_copy, 3)
+        stage_q(0)
+        spread_ab()
+        stage_e(1)
+        w_quant(2)
+        w_quant(3)
+        stage_m(0)
+        stage_r(2)
+        stage_t(2)
+        copy_ab()
+
+        for k in range(NT):
+            stage_ab(k, 0)
+            stage_ab(k, 1)
+            if k >= 1:
+                stage_eps(k - 1)
+            if k + 1 < NT:
+                stage_q(k + 1)
+                stage_m(k + 1)
+            stage_n(k)
+            stage_p2(k)
+            if k >= 1:
+                stage_rec(k - 1)
+                stage_side(k - 1)
+            stage_p3(k)
+            if k >= 1:
+                stage_p45(k - 1, 1)
+            if k + 2 < NT:
+                stage_e(k + 2)
+            stage_sqrt(k)
+            if k + 3 < NT:
+                stage_r(k + 3)
+                stage_t(k + 3)
+            if k >= 1:
+                stage_cast(k - 1)
+            if k >= 2:
+                stage_side_out(k - 2)
+        stage_eps(NT - 1)
+        stage_side_out(NT - 2)
+        stage_rec(NT - 1)
+        stage_p45(NT - 1, 2)

@@ -215,13 +215,14 @@ def tile_multiheadattention_pa_kernel(tc, attn_out, inp, w_proj1, w_proj2, ln_a,
         def stage_sqrt(j):
             nc.scalar.activation(out=ss_t[j][:, 1:2], in_=ss_t[j][:, 0:1], func=ACT.Sqrt, scale=1.0 / (N - 1))
 
-        def stage_p3(j):
-            wv = N - share(j)
-            t = work.tile([P, N], F32, name="t")
+        def stage_p3(j, c0=0, c1=None):
+            if c1 is None:
+                c1 = N - share(j)
+            if c0 == 0:
+                t_t[j] = work.tile([P, N], F32, name="t")
             nc.vector.scalar_tensor_tensor(
-                out=t[:, 0:wv], in0=z_t[j][:, 0:wv], scalar=sv_t[j][:, 2:3], in1=a_ps[:, 0:wv], op0=ALU.add, op1=ALU.mult
+                out=t_t[j][:, c0:c1], in0=z_t[j][:, c0:c1], scalar=sv_t[j][:, 2:3], in1=a_ps[:, c0:c1], op0=ALU.add, op1=ALU.mult
             )
-            t_t[j] = t
 
         def stage_eps(j):
             nc.vector.tensor_scalar(out=sv_t[j][:, 3:4], in0=ss_t[j][:, 1:2], scalar1=EPS, scalar2=None, op0=ALU.add)
@@ -243,19 +244,22 @@ def tile_multiheadattention_pa_kernel(tc, attn_out, inp, w_proj1, w_proj2, ln_a,
             og_t[j] = og
 
         def stage_p45(j, pieces):
-            wv = N - share(j)
             o = work.tile([P, N], F32, name="o")
             o8 = work.tile([P, N], FP8, name="o8")
             o8_t[j] = o8
-            w = wv // pieces
-            for k in range(pieces):
-                cols = slice(w * k, w * (k + 1))
+            for k in range(len(pieces) - 1):
+                cols = slice(pieces[k], pieces[k + 1])
                 nc.vector.scalar_tensor_tensor(
                     out=o[:, cols], in0=t_t[j][:, cols], scalar=sv_t[j][:, 4:5], in1=b_ps[:, cols], op0=ALU.mult, op1=ALU.add
                 )
                 nc.sync.dma_start(out=out_rows(out_0, j)[:, cols], in_=o[:, cols])
-                if share(j) == 0:
+                if share(j) == 0 and k < len(pieces) - 2:
                     nc.scalar.activation(out=o8[:, cols], in_=o[:, cols], func=ACT.Copy, scale=Y_SCALE, saturate=False)
+                    nc.sync.dma_start(out=out_rows(out_1, j)[:, cols], in_=o8[:, cols].bitcast(U8))
+                if share(j) == 0 and k == len(pieces) - 2:
+                    nc.vector.tensor_scalar(
+                        out=o8[:, cols], in0=o[:, cols], scalar1=Y_SCALE, scalar2=None, op0=ALU.mult, saturate=False
+                    )
                     nc.sync.dma_start(out=out_rows(out_1, j)[:, cols], in_=o8[:, cols].bitcast(U8))
             o_t[j] = o
 
@@ -303,20 +307,29 @@ def tile_multiheadattention_pa_kernel(tc, attn_out, inp, w_proj1, w_proj2, ln_a,
             if k >= 1:
                 stage_rec(k - 1)
                 stage_side(k - 1)
-            stage_p3(k)
-            if k >= 1:
-                stage_p45(k - 1, 1)
+            if k < NT - 1:
+                stage_p3(k)
+                if k >= 1:
+                    stage_p45(k - 1, [0, C0])
+            else:
+                stage_p3(k, 0, 512)
+                stage_p45(k - 1, [0, C0])
             if k + 2 < NT:
                 stage_e(k + 2)
             stage_sqrt(k)
             if k + 3 < NT:
                 stage_r(k + 3)
                 stage_t(k + 3)
-            if k >= 1:
-                stage_cast(k - 1)
-            if k >= 2:
+            if k < NT - 1:
+                if k >= 1:
+                    stage_cast(k - 1)
+                if k >= 2:
+                    stage_side_out(k - 2)
+            else:
                 stage_side_out(k - 2)
+                stage_cast(k - 1)
         stage_eps(NT - 1)
+        stage_p3(NT - 1, 512, N)
         stage_side_out(NT - 2)
         stage_rec(NT - 1)
-        stage_p45(NT - 1, 2)
+        stage_p45(NT - 1, [0, 512, 768, N])

@@ -46,10 +46,22 @@ def tile_multiheadattention_pa_kernel(tc, attn_out, inp, w_proj1, w_proj2, ln_a,
         nc.vector.memset(warm[:], 1.0)
         nc.vector.memset(ab_row[:], 0.0)
         nc.vector.memset(ones[:], 1.0)
+        ones_nt = keep.tile([P, NT], F32, name="ones_nt")
+        sq_eps = keep.tile([P, 2 * NT], F32, name="sq_eps")
+        sig_eps = keep.tile([P, NT], F32, name="sig_eps")
+        nc.vector.memset(ones_nt[:], 1.0)
+        nc.vector.tensor_scalar(
+            out=sq_eps[:].rearrange("p (j two) -> p j two", two=2)[:, :, 1],
+            in0=ones_nt[:],
+            scalar1=EPS * EPS * (N - 1),
+            scalar2=None,
+            op0=ALU.mult,
+        )
         nc.scalar.activation(out=warm2[:], in_=warm[:], func=ACT.Sqrt)
         make_identity(nc, ident[:])
 
         x_raw = {}
+        x_split = {}
         inp_sb = {}
         w_raw = {}
 
@@ -57,6 +69,13 @@ def tile_multiheadattention_pa_kernel(tc, attn_out, inp, w_proj1, w_proj2, ln_a,
             t = loads.tile([P, H, 256], BF16, name="x_raw")
             nc.sync.dma_start(out=t[:], in_=attn[:, 256 * c : 256 * (c + 1), :].rearrange("h (p i) f -> p h (i f)", i=2))
             x_raw[c] = t
+
+        def load_x_split(c):
+            t = loads.tile([P, 4, 512], BF16, name="x_split")
+            rows = attn[:, 256 * c : 256 * (c + 1), :].rearrange("h (p i) (f e) -> p i f h e", i=2, f=2)
+            for g in range(4):
+                nc.sync.dma_start(out=t[:, g, :].rearrange("p (h e) -> p h e", e=64), in_=rows[:, g // 2, g % 2])
+            x_split[c] = t
 
         def load_inp(c):
             t = loads.tile([P, 2 * N], BF16, name="inp_sb")
@@ -75,8 +94,10 @@ def tile_multiheadattention_pa_kernel(tc, attn_out, inp, w_proj1, w_proj2, ln_a,
         nc.sync.dma_start(out=ab_row[0:1, 0:N], in_=ln_a.rearrange("(o n) -> o n", o=1))
         nc.sync.dma_start(out=ab_row[0:1, N : 2 * N], in_=ln_b.rearrange("(o n) -> o n", o=1))
         load_inp(0)
-        for c in range(1, 4):
-            load_x(c)
+        load_x(1)
+        load_inp(1)
+        for c in range(2, 4):
+            load_x_split(c)
             load_inp(c)
 
         a_ps = ps_const.tile([P, N], BF16, name="a_ps")
@@ -121,7 +142,6 @@ def tile_multiheadattention_pa_kernel(tc, attn_out, inp, w_proj1, w_proj2, ln_a,
         acc_t = {}
         z_t = {}
         sv_t = {}
-        ss_t = {}
         t_t = {}
         og_t = {}
         o_t = {}
@@ -136,14 +156,17 @@ def tile_multiheadattention_pa_kernel(tc, attn_out, inp, w_proj1, w_proj2, ln_a,
 
         def stage_r(j):
             c, i = divmod(j, 2)
+            if c >= 2:
+                xs_t[j] = x_split[c][:, 2 * i : 2 * i + 2, :].rearrange("p g x -> p (g x)")
+                return
             xs = work.tile([P, 1024], BF16, name="xs")
             xw = x_raw[c][:].bitcast(F32).rearrange("p h (i f v) -> p i f h v", i=2, f=2)
             nc.scalar.copy(out=xs[:].bitcast(F32).rearrange("p (f h v) -> p f h v", f=2, h=H), in_=xw[:, i])
-            xs_t[j] = xs
+            xs_t[j] = xs[:]
 
         def stage_t(j):
             xt = ps_t.tile([P, 4, P], F32, name="xt")
-            xw = xs_t[j][:].bitcast(F32)
+            xw = xs_t[j].bitcast(F32)
             for f in range(2):
                 for u in range(2):
                     nc.tensor.transpose(xt[:, 2 * f + u, :], xw[:, 256 * f + u : 256 * (f + 1) : 2], ident[:])
@@ -206,14 +229,24 @@ def tile_multiheadattention_pa_kernel(tc, attn_out, inp, w_proj1, w_proj2, ln_a,
 
         def stage_p2(j):
             junk = work.tile([P, N], BF16, name="junk")
-            ss = stats.tile([P, 8], F32, name="ss")
             nc.scalar.activation(
-                out=junk[:], in_=z_t[j][:], func=ACT.Square, bias=sv_t[j][:, 2:3], scale=1.0, accum_out=ss[:, 0:1]
+                out=junk[:],
+                in_=z_t[j][:],
+                func=ACT.Square,
+                bias=sv_t[j][:, 2:3],
+                scale=1.0,
+                accum_out=sq_eps[:, 2 * j : 2 * j + 1],
             )
-            ss_t[j] = ss
 
         def stage_sqrt(j):
-            nc.scalar.activation(out=ss_t[j][:, 1:2], in_=ss_t[j][:, 0:1], func=ACT.Sqrt, scale=1.0 / (N - 1))
+            ss = stats.tile([P, 8], F32, name="ss")
+            nc.scalar.activation(
+                out=ss[:, 0:2],
+                in_=sq_eps[:, 2 * j : 2 * j + 2],
+                func=ACT.Sqrt,
+                scale=1.0 / (N - 1),
+                accum_out=sig_eps[:, j : j + 1],
+            )
 
         def stage_p3(j, c0=0, c1=None):
             if c1 is None:
@@ -224,11 +257,8 @@ def tile_multiheadattention_pa_kernel(tc, attn_out, inp, w_proj1, w_proj2, ln_a,
                 out=t_t[j][:, c0:c1], in0=z_t[j][:, c0:c1], scalar=sv_t[j][:, 2:3], in1=a_ps[:, c0:c1], op0=ALU.add, op1=ALU.mult
             )
 
-        def stage_eps(j):
-            nc.vector.tensor_scalar(out=sv_t[j][:, 3:4], in0=ss_t[j][:, 1:2], scalar1=EPS, scalar2=None, op0=ALU.add)
-
         def stage_rec(j):
-            nc.vector.reciprocal(out=sv_t[j][:, 4:5], in_=sv_t[j][:, 3:4])
+            nc.vector.reciprocal(out=sv_t[j][:, 4:5], in_=sig_eps[:, j : j + 1])
 
         def stage_side(j):
             if share(j) == 0:
@@ -297,8 +327,6 @@ def tile_multiheadattention_pa_kernel(tc, attn_out, inp, w_proj1, w_proj2, ln_a,
         for k in range(NT):
             stage_ab(k, 0)
             stage_ab(k, 1)
-            if k >= 1:
-                stage_eps(k - 1)
             if k + 1 < NT:
                 stage_q(k + 1)
                 stage_m(k + 1)
@@ -328,7 +356,6 @@ def tile_multiheadattention_pa_kernel(tc, attn_out, inp, w_proj1, w_proj2, ln_a,
             else:
                 stage_side_out(k - 2)
                 stage_cast(k - 1)
-        stage_eps(NT - 1)
         stage_p3(NT - 1, 512, N)
         stage_side_out(NT - 2)
         stage_rec(NT - 1)

@@ -142,6 +142,7 @@ def tile_multiheadattention_pa_kernel(tc, attn_out, inp, w_proj1, w_proj2, ln_a,
         acc_t = {}
         z_t = {}
         sv_t = {}
+        neg_t = {}
         t_t = {}
         og_t = {}
         o_t = {}
@@ -226,6 +227,12 @@ def tile_multiheadattention_pa_kernel(tc, attn_out, inp, w_proj1, w_proj2, ln_a,
             nc.vector.tensor_scalar(
                 out=sv[:, 2:3], in0=sv[:, 0:1], scalar1=sv[:, 1:2], scalar2=-1.0 / N, op0=ALU.add, op1=ALU.mult
             )
+            neg_t[j] = sv[:, 2:3]
+
+        def stage_n_scalar(j):
+            nj = stats.tile([P, 8], F32, name="nj")
+            nc.scalar.activation(out=nj[:, 0:2], in_=sv_t[j][:, 0:2], func=ACT.Copy, scale=-1.0 / N, accum_out=nj[:, 2:3])
+            neg_t[j] = nj[:, 2:3]
 
         def stage_p2(j):
             junk = work.tile([P, N], BF16, name="junk")
@@ -233,7 +240,7 @@ def tile_multiheadattention_pa_kernel(tc, attn_out, inp, w_proj1, w_proj2, ln_a,
                 out=junk[:],
                 in_=z_t[j][:],
                 func=ACT.Square,
-                bias=sv_t[j][:, 2:3],
+                bias=neg_t[j],
                 scale=1.0,
                 accum_out=sq_eps[:, 2 * j : 2 * j + 1],
             )
@@ -254,7 +261,7 @@ def tile_multiheadattention_pa_kernel(tc, attn_out, inp, w_proj1, w_proj2, ln_a,
             if c0 == 0:
                 t_t[j] = work.tile([P, N], F32, name="t")
             nc.vector.scalar_tensor_tensor(
-                out=t_t[j][:, c0:c1], in0=z_t[j][:, c0:c1], scalar=sv_t[j][:, 2:3], in1=a_ps[:, c0:c1], op0=ALU.add, op1=ALU.mult
+                out=t_t[j][:, c0:c1], in0=z_t[j][:, c0:c1], scalar=neg_t[j], in1=a_ps[:, c0:c1], op0=ALU.add, op1=ALU.mult
             )
 
         def stage_rec(j):
@@ -265,7 +272,7 @@ def tile_multiheadattention_pa_kernel(tc, attn_out, inp, w_proj1, w_proj2, ln_a,
                 return
             u = work.tile([P, CW], F32, name="u")
             nc.gpsimd.tensor_scalar(
-                out=u[:], in0=z_t[j][:, C0:N], scalar1=sv_t[j][:, 2:3], scalar2=sv_t[j][:, 4:5], op0=ALU.add, op1=ALU.mult
+                out=u[:], in0=z_t[j][:, C0:N], scalar1=neg_t[j], scalar2=sv_t[j][:, 4:5], op0=ALU.add, op1=ALU.mult
             )
             v = work.tile([P, CW], F32, name="v")
             og = work.tile([P, CW], F32, name="og")
@@ -325,20 +332,27 @@ def tile_multiheadattention_pa_kernel(tc, attn_out, inp, w_proj1, w_proj2, ln_a,
         copy_ab()
 
         for k in range(NT):
+            last = k == NT - 1
             stage_ab(k, 0)
             stage_ab(k, 1)
-            if k + 1 < NT:
-                stage_q(k + 1)
-                stage_m(k + 1)
-            stage_n(k)
-            stage_p2(k)
             if k >= 1:
                 stage_rec(k - 1)
+            if not last:
+                stage_q(k + 1)
+                stage_m(k + 1)
+            if k == 0 or last:
+                stage_n(k)
+            else:
+                stage_n_scalar(k)
+            if k >= 2 and not last:
+                stage_side_out(k - 2)
+            stage_p2(k)
+            if k >= 1:
                 stage_side(k - 1)
-            if k < NT - 1:
-                stage_p3(k)
+            if not last:
                 if k >= 1:
                     stage_p45(k - 1, [0, C0])
+                stage_p3(k)
             else:
                 stage_p3(k, 0, 512)
                 stage_p45(k - 1, [0, C0])
@@ -348,13 +362,9 @@ def tile_multiheadattention_pa_kernel(tc, attn_out, inp, w_proj1, w_proj2, ln_a,
             if k + 3 < NT:
                 stage_r(k + 3)
                 stage_t(k + 3)
-            if k < NT - 1:
-                if k >= 1:
-                    stage_cast(k - 1)
-                if k >= 2:
-                    stage_side_out(k - 2)
-            else:
+            if last:
                 stage_side_out(k - 2)
+            if k >= 1:
                 stage_cast(k - 1)
         stage_p3(NT - 1, 512, N)
         stage_side_out(NT - 2)

@@ -290,10 +290,12 @@ def tile_multiheadattention_pa_kernel(tc, attn_out, inp, w_proj1, w_proj2, ln_a,
                     out=o[:, cols], in0=t_t[j][:, cols], scalar=sv_t[j][:, 4:5], in1=b_ps[:, cols], op0=ALU.mult, op1=ALU.add
                 )
                 nc.sync.dma_start(out=out_rows(out_0, j)[:, cols], in_=o[:, cols])
-                if share(j) == 0 and k < len(pieces) - 2:
+                if share(j) == 0 and k == 0:
                     nc.scalar.activation(out=o8[:, cols], in_=o[:, cols], func=ACT.Copy, scale=Y_SCALE, saturate=False)
                     nc.sync.dma_start(out=out_rows(out_1, j)[:, cols], in_=o8[:, cols].bitcast(U8))
-                if share(j) == 0 and k == len(pieces) - 2:
+            if share(j) == 0:
+                for k in range(1, len(pieces) - 1):
+                    cols = slice(pieces[k], pieces[k + 1])
                     nc.vector.tensor_scalar(
                         out=o8[:, cols], in0=o[:, cols], scalar1=Y_SCALE, scalar2=None, op0=ALU.mult, saturate=False
                     )
@@ -331,42 +333,44 @@ def tile_multiheadattention_pa_kernel(tc, attn_out, inp, w_proj1, w_proj2, ln_a,
         stage_t(2)
         copy_ab()
 
-        for k in range(NT):
-            last = k == NT - 1
+        for k in range(NT - 1):
             stage_ab(k, 0)
             stage_ab(k, 1)
             if k >= 1:
                 stage_rec(k - 1)
-            if not last:
-                stage_q(k + 1)
-                stage_m(k + 1)
-            if k == 0 or last:
+            stage_q(k + 1)
+            stage_m(k + 1)
+            if k == 0:
                 stage_n(k)
             else:
                 stage_n_scalar(k)
-            if k >= 2 and not last:
+            if k >= 2:
                 stage_side_out(k - 2)
             stage_p2(k)
             if k >= 1:
                 stage_side(k - 1)
-            if not last:
-                if k >= 1:
-                    stage_p45(k - 1, [0, C0])
-                stage_p3(k)
-            else:
-                stage_p3(k, 0, 512)
                 stage_p45(k - 1, [0, C0])
+            stage_p3(k)
             if k + 2 < NT:
                 stage_e(k + 2)
             stage_sqrt(k)
             if k + 3 < NT:
                 stage_r(k + 3)
                 stage_t(k + 3)
-            if last:
-                stage_side_out(k - 2)
             if k >= 1:
                 stage_cast(k - 1)
+        stage_ab(NT - 1, 0)
+        stage_rec(NT - 2)
+        stage_ab(NT - 1, 1)
+        stage_n(NT - 1)
+        stage_side_out(NT - 3)
+        stage_p2(NT - 1)
+        stage_side(NT - 2)
+        stage_p45(NT - 2, [0, C0])
+        stage_p3(NT - 1, 0, 512)
+        stage_sqrt(NT - 1)
+        stage_cast(NT - 2)
+        stage_rec(NT - 1)
         stage_p3(NT - 1, 512, N)
         stage_side_out(NT - 2)
-        stage_rec(NT - 1)
         stage_p45(NT - 1, [0, 512, 768, N])

@@ -18,7 +18,7 @@ N = 1024
 NT = 8
 EPS = 1e-3
 Y_SCALE = 220.0
-CW = 320
+CW = 352
 C0 = N - CW
 
 FLOPS = 2 * 1024 * 512 * 1024

@@ -275,14 +275,14 @@ def tile_multiheadattention_pa_kernel(tc, attn_out, inp, w_proj1, w_proj2, ln_a,
                 out=u[:], in0=z_t[j][:, C0:N], scalar1=neg_t[j], scalar2=sv_t[j][:, 4:5], op0=ALU.add, op1=ALU.mult
             )
             v = work.tile([P, CW], F32, name="v")
-            og = work.tile([P, CW], F32, name="og")
+            og = work.tile([P, CW], F32, name="og", bufs=8)
             nc.gpsimd.tensor_tensor(out=v[:], in0=u[:], in1=a_sb[:, 0:CW], op=ALU.mult)
             nc.gpsimd.tensor_tensor(out=og[:], in0=v[:], in1=b_sb[:, 0:CW], op=ALU.add)
             og_t[j] = og
 
         def stage_p45(j, pieces):
-            o = work.tile([P, N], F32, name="o")
-            o8 = work.tile([P, N], FP8, name="o8")
+            o = work.tile([P, N], F32, name="o", bufs=8)
+            o8 = work.tile([P, N], FP8, name="o8", bufs=8)
             o8_t[j] = o8
             for k in range(len(pieces) - 1):
                 cols = slice(pieces[k], pieces[k + 1])

@@ -40,12 +40,16 @@ def tile_multiheadattention_pa_kernel(tc, attn_out, inp, w_proj1, w_proj2, ln_a,
 
         warm = keep.tile([P, 1], F32, name="warm")
         warm2 = keep.tile([P, 1], F32, name="warm2")
-        ab_row = keep.tile([P, 2 * N], BF16, name="ab_row")
-        ones = keep.tile([P, P], BF16, name="ones")
+        ab_row = keep.tile([P, N], BF16, name="ab_row")
+        pick_a = keep.tile([P, P], BF16, name="pick_a")
+        pick_b = keep.tile([P, P], BF16, name="pick_b")
         ident = keep.tile([P, P], F32, name="ident")
+        nc.vector.memset(ab_row[:].bitcast(U32), 0)
         nc.vector.memset(warm[:], 1.0)
-        nc.vector.memset(ab_row[:], 0.0)
-        nc.vector.memset(ones[:], 1.0)
+        nc.vector.memset(pick_a[:].bitcast(U32), 0)
+        nc.vector.memset(pick_b[:].bitcast(U32), 0)
+        nc.vector.memset(pick_a[0:1, :], 1.0)
+        nc.vector.memset(pick_b[32:33, :], 1.0)
         ones_nt = keep.tile([P, NT], F32, name="ones_nt")
         sq_eps = keep.tile([P, 2 * NT], F32, name="sq_eps")
         sig_eps = keep.tile([P, NT], F32, name="sig_eps")
@@ -57,6 +61,8 @@ def tile_multiheadattention_pa_kernel(tc, attn_out, inp, w_proj1, w_proj2, ln_a,
             scalar2=None,
             op0=ALU.mult,
         )
+        nc.scalar.dma_start(out=ab_row[0:1, :], in_=ln_a.rearrange("(o n) -> o n", o=1))
+        nc.scalar.dma_start(out=ab_row[32:33, :], in_=ln_b.rearrange("(o n) -> o n", o=1))
         nc.scalar.activation(out=warm2[:], in_=warm[:], func=ACT.Sqrt)
         make_identity(nc, ident[:])
 
@@ -80,7 +86,13 @@ def tile_multiheadattention_pa_kernel(tc, attn_out, inp, w_proj1, w_proj2, ln_a,
         def load_inp(c):
             t = loads.tile([P, 2 * N], BF16, name="inp_sb")
             nc.sync.dma_start(out=t[:], in_=inp[256 * c : 256 * (c + 1), :].rearrange("(p i) n -> p (i n)", i=2))
-            inp_sb[c] = t
+            inp_sb[2 * c] = t[:, 0:N]
+            inp_sb[2 * c + 1] = t[:, N : 2 * N]
+
+        def load_inp_tile(i):
+            t = loads.tile([P, N], BF16, name="inp_first", bufs=2)
+            nc.sync.dma_start(out=t[:], in_=inp[0:256, :].rearrange("(p i) n -> p i n", i=2)[:, i, :])
+            inp_sb[i] = t[:]
 
         def load_w(c):
             t = loads.tile([P, 4, 256], BF16, name="w_raw")
@@ -91,10 +103,9 @@ def tile_multiheadattention_pa_kernel(tc, attn_out, inp, w_proj1, w_proj2, ln_a,
         load_x(0)
         for c in range(4):
             load_w(c)
-        nc.sync.dma_start(out=ab_row[0:1, 0:N], in_=ln_a.rearrange("(o n) -> o n", o=1))
-        nc.sync.dma_start(out=ab_row[0:1, N : 2 * N], in_=ln_b.rearrange("(o n) -> o n", o=1))
-        load_inp(0)
+        load_inp_tile(0)
         load_x(1)
+        load_inp_tile(1)
         load_inp(1)
         for c in range(2, 4):
             load_x_split(c)
@@ -108,10 +119,10 @@ def tile_multiheadattention_pa_kernel(tc, attn_out, inp, w_proj1, w_proj2, ln_a,
         def spread_ab():
             for half in range(2):
                 cols = slice(512 * half, 512 * (half + 1))
-                nc.tensor.matmul(out=a_ps[:, cols], lhsT=ones[:], rhs=ab_row[:, 512 * half : 512 * (half + 1)], start=True, stop=True)
+                nc.tensor.matmul(out=a_ps[:, cols], lhsT=pick_a[:], rhs=ab_row[:, 512 * half : 512 * (half + 1)], start=True, stop=True)
             for half in range(2):
                 cols = slice(512 * half, 512 * (half + 1))
-                nc.tensor.matmul(out=b_ps[:, cols], lhsT=ones[:], rhs=ab_row[:, N + 512 * half : N + 512 * (half + 1)], start=True, stop=True)
+                nc.tensor.matmul(out=b_ps[:, cols], lhsT=pick_b[:], rhs=ab_row[:, 512 * half : 512 * (half + 1)], start=True, stop=True)
 
         def copy_ab():
             if CW > 0:
@@ -208,7 +219,6 @@ def tile_multiheadattention_pa_kernel(tc, attn_out, inp, w_proj1, w_proj2, ln_a,
             acc_t[j] = (acc0, acc1)
 
         def stage_ab(j, b):
-            c, i = divmod(j, 2)
             if b == 0:
                 z_t[j] = work.tile([P, N], F32, name="z")
                 sv_t[j] = stats.tile([P, 8], F32, name="sv")
@@ -216,7 +226,7 @@ def tile_multiheadattention_pa_kernel(tc, attn_out, inp, w_proj1, w_proj2, ln_a,
                 out=z_t[j][:, 512 * b : 512 * (b + 1)],
                 in0=acc_t[j][b][:],
                 scalar=1.0,
-                in1=inp_sb[c][:, N * i + 512 * b : N * i + 512 * (b + 1)],
+                in1=inp_sb[j][:, 512 * b : 512 * (b + 1)],
                 op0=ALU.mult,
                 op1=ALU.add,
                 accum_out=sv_t[j][:, b : b + 1],
@@ -312,6 +322,7 @@ def tile_multiheadattention_pa_kernel(tc, attn_out, inp, w_proj1, w_proj2, ln_a,
             nc.scalar.activation(out=o8_t[j][:, C0:N], in_=og_t[j][:], func=ACT.Copy, scale=Y_SCALE, saturate=False)
             nc.sync.dma_start(out=out_rows(out_1, j), in_=o8_t[j][:].bitcast(U8))
 
+        spread_ab()
         stage_r(0)
         stage_r(1)
         stage_t(0)
@@ -324,7 +335,6 @@ def tile_multiheadattention_pa_kernel(tc, attn_out, inp, w_proj1, w_proj2, ln_a,
         w_quant(1)
         w_interleave(nc.vector.tensor_copy, 3)
         stage_q(0)
-        spread_ab()
         stage_e(1)
         w_quant(2)
         w_quant(3)

@@ -61,8 +61,6 @@ def tile_multiheadattention_pa_kernel(tc, attn_out, inp, w_proj1, w_proj2, ln_a,
             scalar2=None,
             op0=ALU.mult,
         )
-        nc.scalar.dma_start(out=ab_row[0:1, :], in_=ln_a.rearrange("(o n) -> o n", o=1))
-        nc.scalar.dma_start(out=ab_row[32:33, :], in_=ln_b.rearrange("(o n) -> o n", o=1))
         nc.scalar.activation(out=warm2[:], in_=warm[:], func=ACT.Sqrt)
         make_identity(nc, ident[:])
 
@@ -101,6 +99,8 @@ def tile_multiheadattention_pa_kernel(tc, attn_out, inp, w_proj1, w_proj2, ln_a,
             w_raw[c] = t
 
         load_x(0)
+        nc.sync.dma_start(out=ab_row[0:1, :], in_=ln_a.rearrange("(o n) -> o n", o=1))
+        nc.sync.dma_start(out=ab_row[32:33, :], in_=ln_b.rearrange("(o n) -> o n", o=1))
         for c in range(4):
             load_w(c)
         load_inp_tile(0)
@@ -172,8 +172,8 @@ def tile_multiheadattention_pa_kernel(tc, attn_out, inp, w_proj1, w_proj2, ln_a,
                 xs_t[j] = x_split[c][:, 2 * i : 2 * i + 2, :].rearrange("p g x -> p (g x)")
                 return
             xs = work.tile([P, 1024], BF16, name="xs")
-            xw = x_raw[c][:].bitcast(F32).rearrange("p h (i f v) -> p i f h v", i=2, f=2)
-            nc.scalar.copy(out=xs[:].bitcast(F32).rearrange("p (f h v) -> p f h v", f=2, h=H), in_=xw[:, i])
+            xw = x_raw[c][:].bitcast(F32).rearrange("p h (i f q u) -> p i f u h q", i=2, f=2, u=2)
+            nc.scalar.copy(out=xs[:].bitcast(F32).rearrange("p (f u h q) -> p f u h q", f=2, u=2, h=H), in_=xw[:, i])
             xs_t[j] = xs[:]
 
         def stage_t(j):
@@ -181,7 +181,9 @@ def tile_multiheadattention_pa_kernel(tc, attn_out, inp, w_proj1, w_proj2, ln_a,
             xw = xs_t[j].bitcast(F32)
             for f in range(2):
                 for u in range(2):
-                    nc.tensor.transpose(xt[:, 2 * f + u, :], xw[:, 256 * f + u : 256 * (f + 1) : 2], ident[:])
+                    b = 2 * f + u
+                    words = xw[:, P * b : P * (b + 1)] if j < 4 else xw[:, 256 * f + u : 256 * (f + 1) : 2]
+                    nc.tensor.transpose(xt[:, b, :], words, ident[:])
             xt_t[j] = xt
 
         def stage_e(j):
@@ -322,7 +324,6 @@ def tile_multiheadattention_pa_kernel(tc, attn_out, inp, w_proj1, w_proj2, ln_a,
             nc.scalar.activation(out=o8_t[j][:, C0:N], in_=og_t[j][:], func=ACT.Copy, scale=Y_SCALE, saturate=False)
             nc.sync.dma_start(out=out_rows(out_1, j), in_=o8_t[j][:].bitcast(U8))
 
-        spread_ab()
         stage_r(0)
         stage_r(1)
         stage_t(0)
@@ -335,6 +336,7 @@ def tile_multiheadattention_pa_kernel(tc, attn_out, inp, w_proj1, w_proj2, ln_a,
         w_quant(1)
         w_interleave(nc.vector.tensor_copy, 3)
         stage_q(0)
+        spread_ab()
         stage_e(1)
         w_quant(2)
         w_quant(3)

@@ -19,7 +19,7 @@ NT = 8
 EPS = 1e-3
 Y_SCALE = 220.0
 CW = 352
-C0 = N - CW
+CW_LAST = 256
 
 FLOPS = 2 * 1024 * 512 * 1024
 
@@ -113,8 +113,8 @@ def tile_multiheadattention_pa_kernel(tc, attn_out, inp, w_proj1, w_proj2, ln_a,
 
         a_ps = ps_const.tile([P, N], BF16, name="a_ps")
         b_ps = ps_const.tile([P, N], BF16, name="b_ps")
-        a_sb = keep.tile([P, max(CW, 64)], BF16, name="a_sb")
-        b_sb = keep.tile([P, max(CW, 64)], BF16, name="b_sb")
+        a_sb = keep.tile([P, CW], BF16, name="a_sb")
+        b_sb = keep.tile([P, CW], BF16, name="b_sb")
 
         def spread_ab():
             for half in range(2):
@@ -126,8 +126,8 @@ def tile_multiheadattention_pa_kernel(tc, attn_out, inp, w_proj1, w_proj2, ln_a,
 
         def copy_ab():
             if CW > 0:
-                nc.scalar.copy(out=a_sb[:, 0:CW], in_=a_ps[:, C0:N])
-                nc.scalar.copy(out=b_sb[:, 0:CW], in_=b_ps[:, C0:N])
+                nc.scalar.copy(out=a_sb[:, 0:CW], in_=a_ps[:, N - CW : N])
+                nc.scalar.copy(out=b_sb[:, 0:CW], in_=b_ps[:, N - CW : N])
 
         w_g = keep.tile([P, 4 * N], BF16, name="w_g", align_bytes=64)
         w_c = keep.tile([P, N], U32, name="w_c", align_bytes=64)
@@ -160,7 +160,7 @@ def tile_multiheadattention_pa_kernel(tc, attn_out, inp, w_proj1, w_proj2, ln_a,
         o8_t = {}
 
         def share(j):
-            return CW if j < NT - 1 else 0
+            return CW if j < NT - 2 else CW_LAST if j == NT - 2 else 0
 
         def out_rows(dram, j):
             c, i = divmod(j, 2)
@@ -282,14 +282,15 @@ def tile_multiheadattention_pa_kernel(tc, attn_out, inp, w_proj1, w_proj2, ln_a,
         def stage_side(j):
             if share(j) == 0:
                 return
+            w = share(j)
             u = work.tile([P, CW], F32, name="u")
             nc.gpsimd.tensor_scalar(
-                out=u[:], in0=z_t[j][:, C0:N], scalar1=neg_t[j], scalar2=sv_t[j][:, 4:5], op0=ALU.add, op1=ALU.mult
+                out=u[:, 0:w], in0=z_t[j][:, N - w : N], scalar1=neg_t[j], scalar2=sv_t[j][:, 4:5], op0=ALU.add, op1=ALU.mult
             )
             v = work.tile([P, CW], F32, name="v")
             og = work.tile([P, CW], F32, name="og", bufs=8)
-            nc.gpsimd.tensor_tensor(out=v[:], in0=u[:], in1=a_sb[:, 0:CW], op=ALU.mult)
-            nc.gpsimd.tensor_tensor(out=og[:], in0=v[:], in1=b_sb[:, 0:CW], op=ALU.add)
+            nc.gpsimd.tensor_tensor(out=v[:, 0:w], in0=u[:, 0:w], in1=a_sb[:, CW - w : CW], op=ALU.mult)
+            nc.gpsimd.tensor_tensor(out=og[:, 0:w], in0=v[:, 0:w], in1=b_sb[:, CW - w : CW], op=ALU.add)
             og_t[j] = og
 
         def stage_p45(j, pieces):
@@ -302,26 +303,40 @@ def tile_multiheadattention_pa_kernel(tc, attn_out, inp, w_proj1, w_proj2, ln_a,
                     out=o[:, cols], in0=t_t[j][:, cols], scalar=sv_t[j][:, 4:5], in1=b_ps[:, cols], op0=ALU.mult, op1=ALU.add
                 )
                 nc.sync.dma_start(out=out_rows(out_0, j)[:, cols], in_=o[:, cols])
-                if share(j) == 0 and k == 0:
+            o_t[j] = o
+
+        def stage_last(j, pieces):
+            stage_p45(j, pieces)
+            o, o8 = o_t[j], o8_t[j]
+            stage_bytes(j - 1)
+            for k in range(len(pieces) - 1):
+                cols = slice(pieces[k], pieces[k + 1])
+                if k == 0:
                     nc.scalar.activation(out=o8[:, cols], in_=o[:, cols], func=ACT.Copy, scale=Y_SCALE, saturate=False)
-                    nc.sync.dma_start(out=out_rows(out_1, j)[:, cols], in_=o8[:, cols].bitcast(U8))
-            if share(j) == 0:
-                for k in range(1, len(pieces) - 1):
-                    cols = slice(pieces[k], pieces[k + 1])
+                else:
                     nc.vector.tensor_scalar(
                         out=o8[:, cols], in0=o[:, cols], scalar1=Y_SCALE, scalar2=None, op0=ALU.mult, saturate=False
                     )
-                    nc.sync.dma_start(out=out_rows(out_1, j)[:, cols], in_=o8[:, cols].bitcast(U8))
-            o_t[j] = o
+                nc.sync.dma_start(out=out_rows(out_1, j)[:, cols], in_=o8[:, cols].bitcast(U8))
 
         def stage_cast(j):
-            nc.scalar.activation(out=o8_t[j][:, 0:C0], in_=o_t[j][:, 0:C0], func=ACT.Copy, scale=Y_SCALE, saturate=False)
+            c0 = N - share(j)
+            nc.scalar.activation(out=o8_t[j][:, 0:c0], in_=o_t[j][:, 0:c0], func=ACT.Copy, scale=Y_SCALE, saturate=False)
 
         def stage_side_out(j):
-            if share(j) == 0:
-                return
-            nc.sync.dma_start(out=out_rows(out_0, j)[:, C0:N], in_=og_t[j][:])
-            nc.scalar.activation(out=o8_t[j][:, C0:N], in_=og_t[j][:], func=ACT.Copy, scale=Y_SCALE, saturate=False)
+            stage_side_store(j)
+            stage_side_cast(j)
+            stage_bytes(j)
+
+        def stage_side_store(j):
+            w = share(j)
+            nc.sync.dma_start(out=out_rows(out_0, j)[:, N - w : N], in_=og_t[j][:, 0:w])
+
+        def stage_side_cast(j):
+            w = share(j)
+            nc.scalar.activation(out=o8_t[j][:, N - w : N], in_=og_t[j][:, 0:w], func=ACT.Copy, scale=Y_SCALE, saturate=False)
+
+        def stage_bytes(j):
             nc.sync.dma_start(out=out_rows(out_1, j), in_=o8_t[j][:].bitcast(U8))
 
         stage_r(0)
@@ -361,7 +376,7 @@ def tile_multiheadattention_pa_kernel(tc, attn_out, inp, w_proj1, w_proj2, ln_a,
             stage_p2(k)
             if k >= 1:
                 stage_side(k - 1)
-                stage_p45(k - 1, [0, C0])
+                stage_p45(k - 1, [0, N - share(k - 1)])
             stage_p3(k)
             if k + 2 < NT:
                 stage_e(k + 2)
@@ -377,12 +392,13 @@ def tile_multiheadattention_pa_kernel(tc, attn_out, inp, w_proj1, w_proj2, ln_a,
         stage_n(NT - 1)
         stage_side_out(NT - 3)
         stage_p2(NT - 1)
-        stage_side(NT - 2)
-        stage_p45(NT - 2, [0, C0])
-        stage_p3(NT - 1, 0, 512)
         stage_sqrt(NT - 1)
-        stage_cast(NT - 2)
+        stage_side(NT - 2)
+        stage_p45(NT - 2, [0, N - share(NT - 2)])
+        stage_p3(NT - 1, 0, 768)
         stage_rec(NT - 1)
-        stage_p3(NT - 1, 512, N)
-        stage_side_out(NT - 2)
-        stage_p45(NT - 1, [0, 512, 768, N])
+        stage_p3(NT - 1, 768, N)
+        stage_cast(NT - 2)
+        stage_side_store(NT - 2)
+        stage_side_cast(NT - 2)
+        stage_last(NT - 1, [0, 512, 768, N])

@@ -173,11 +173,36 @@ def tile_multiheadattention_pa_kernel(tc, attn_out, inp, w_proj1, w_proj2, ln_a,
                 return
             xs = work.tile([P, 1024], BF16, name="xs")
             xw = x_raw[c][:].bitcast(F32).rearrange("p h (i f q u) -> p i f u h q", i=2, f=2, u=2)
-            nc.scalar.copy(out=xs[:].bitcast(F32).rearrange("p (f u h q) -> p f u h q", f=2, u=2, h=H), in_=xw[:, i])
+            copy = nc.vector.tensor_copy if j < 2 else nc.scalar.copy
+            copy(out=xs[:].bitcast(F32).rearrange("p (f u h q) -> p f u h q", f=2, u=2, h=H), in_=xw[:, i])
             xs_t[j] = xs[:]
 
+        def stage_t_first():
+            xw = xs_t[0].bitcast(F32)
+            for f in range(2):
+                xt = ps_t.tile([P, 2, P], F32, name="xt")
+                for u in range(2):
+                    b = 2 * f + u
+                    nc.tensor.transpose(xt[:, u, :], xw[:, P * b : P * (b + 1)], ident[:])
+                xt_t[0, f] = xt
+            g_t[0] = work.tile([P, 1024], BF16, name="g", align_bytes=64)
+            xc_t[0] = (work.tile([P, 256], U32, name="xc", align_bytes=64), work.tile([P, 256], U8, name="xsc", align_bytes=64))
+
+        def stage_e_first(f):
+            nc.scalar.copy(
+                out=g_t[0][:, 512 * f : 512 * (f + 1)].bitcast(F32).rearrange("p (r u) -> p r u", u=2),
+                in_=xt_t[0, f][:].rearrange("p u r -> p r u"),
+            )
+
+        def stage_q_first(f):
+            xc, xsc = xc_t[0]
+            nc.vector.quantize_mx(
+                out=xc[:, P * f : P * (f + 1)].bitcast(FP8X4), scales=xsc[:, P * f : P * (f + 1)], in_=g_t[0][:, 512 * f : 512 * (f + 1)]
+            )
+
         def stage_t(j):
-            xt = ps_t.tile([P, 4, P], F32, name="xt")
+            pool, name = (ps_acc, "acc1") if j == 1 else (ps_t, "xt")
+            xt = pool.tile([P, 4, P], F32, name=name)
             xw = xs_t[j].bitcast(F32)
             for f in range(2):
                 for u in range(2):
@@ -341,16 +366,18 @@ def tile_multiheadattention_pa_kernel(tc, attn_out, inp, w_proj1, w_proj2, ln_a,
 
         stage_r(0)
         stage_r(1)
-        stage_t(0)
+        stage_t_first()
         stage_t(1)
         w_interleave(nc.vector.tensor_copy, 0)
         w_interleave(nc.vector.tensor_copy, 1)
-        stage_e(0)
+        stage_e_first(0)
+        stage_e_first(1)
         w_interleave(nc.scalar.copy, 2)
         w_quant(0)
         w_quant(1)
         w_interleave(nc.vector.tensor_copy, 3)
-        stage_q(0)
+        stage_q_first(0)
+        stage_q_first(1)
         spread_ab()
         stage_e(1)
         w_quant(2)

from contextlib import ExitStack

import concourse.mybir as mybir
from concourse.masks import make_identity

F32 = mybir.dt.float32
BF16 = mybir.dt.bfloat16
U32 = mybir.dt.uint32
U8 = mybir.dt.uint8
FP8X4 = mybir.dt.float8_e4m3fn_x4
FP8 = mybir.dt.float8_e4m3fn
ALU = mybir.AluOpType
ACT = mybir.ActivationFunctionType

P = 128
H = 8
N = 1024
NT = 8
EPS = 1e-3
Y_SCALE = 220.0
CW = 352
CW_LAST = 256

FLOPS = 2 * 1024 * 512 * 1024


def tile_multiheadattention_pa_kernel(tc, attn_out, inp, w_proj1, w_proj2, ln_a, ln_b, out_0, out_1):
    nc = tc.nc
    attn = attn_out.rearrange("h b l f -> h (b l) f")

    with ExitStack() as ctx:
        keep = ctx.enter_context(tc.tile_pool(name="keep", bufs=1))
        loads = ctx.enter_context(tc.tile_pool(name="loads", bufs=4))
        work = ctx.enter_context(tc.tile_pool(name="work", bufs=3))
        stats = ctx.enter_context(tc.tile_pool(name="stats", bufs=4))
        ps_const = ctx.enter_context(tc.psum_pool(name="ps_const", bufs=1))
        ps_t = ctx.enter_context(tc.psum_pool(name="ps_t", bufs=2))
        ps_acc = ctx.enter_context(tc.psum_pool(name="ps_acc", bufs=2))
        ctx.enter_context(tc.manual_schedule())

        warm = keep.tile([P, 1], F32, name="warm")
        warm2 = keep.tile([P, 1], F32, name="warm2")
        ab_row = keep.tile([P, N], BF16, name="ab_row")
        pick_a = keep.tile([P, P], BF16, name="pick_a")
        pick_b = keep.tile([P, P], BF16, name="pick_b")
        ident = keep.tile([P, P], F32, name="ident")
        nc.vector.memset(ab_row[:].bitcast(U32), 0)
        nc.vector.memset(warm[:], 1.0)
        nc.vector.memset(pick_a[:].bitcast(U32), 0)
        nc.vector.memset(pick_b[:].bitcast(U32), 0)
        nc.vector.memset(pick_a[0:1, :], 1.0)
        nc.vector.memset(pick_b[32:33, :], 1.0)
        ones_nt = keep.tile([P, NT], F32, name="ones_nt")
        sq_eps = keep.tile([P, 2 * NT], F32, name="sq_eps")
        sig_eps = keep.tile([P, NT], F32, name="sig_eps")
        nc.vector.memset(ones_nt[:], 1.0)
        nc.vector.tensor_scalar(
            out=sq_eps[:].rearrange("p (j two) -> p j two", two=2)[:, :, 1],
            in0=ones_nt[:],
            scalar1=EPS * EPS * (N - 1),
            scalar2=None,
            op0=ALU.mult,
        )
        nc.scalar.activation(out=warm2[:], in_=warm[:], func=ACT.Sqrt)
        make_identity(nc, ident[:])

        x_raw = {}
        x_split = {}
        inp_sb = {}
        w_raw = {}

        def load_x(c):
            t = loads.tile([P, H, 256], BF16, name="x_raw")
            nc.sync.dma_start(out=t[:], in_=attn[:, 256 * c : 256 * (c + 1), :].rearrange("h (p i) f -> p h (i f)", i=2))
            x_raw[c] = t

        def load_x_split(c):
            t = loads.tile([P, 4, 512], BF16, name="x_split")
            rows = attn[:, 256 * c : 256 * (c + 1), :].rearrange("h (p i) (f e) -> p i f h e", i=2, f=2)
            for g in range(4):
                nc.sync.dma_start(out=t[:, g, :].rearrange("p (h e) -> p h e", e=64), in_=rows[:, g // 2, g % 2])
            x_split[c] = t

        def load_inp(c):
            t = loads.tile([P, 2 * N], BF16, name="inp_sb")
            nc.sync.dma_start(out=t[:], in_=inp[256 * c : 256 * (c + 1), :].rearrange("(p i) n -> p (i n)", i=2))
            inp_sb[2 * c] = t[:, 0:N]
            inp_sb[2 * c + 1] = t[:, N : 2 * N]

        def load_inp_tile(i):
            t = loads.tile([P, N], BF16, name="inp_first", bufs=2)
            nc.sync.dma_start(out=t[:], in_=inp[0:256, :].rearrange("(p i) n -> p i n", i=2)[:, i, :])
            inp_sb[i] = t[:]

        def load_w(c):
            t = loads.tile([P, 4, 256], BF16, name="w_raw")
            src = w_proj1[:, 256 * c : 256 * (c + 1)] if c < 3 else w_proj2
            nc.sync.dma_start(out=t[:], in_=src.rearrange("(p j) w -> p j w", j=4))
            w_raw[c] = t

        load_x(0)
        nc.sync.dma_start(out=ab_row[0:1, :], in_=ln_a.rearrange("(o n) -> o n", o=1))
        nc.sync.dma_start(out=ab_row[32:33, :], in_=ln_b.rearrange("(o n) -> o n", o=1))
        for c in range(4):
            load_w(c)
        load_inp_tile(0)
        load_x(1)
        load_inp_tile(1)
        load_inp(1)
        for c in range(2, 4):
            load_x_split(c)
            load_inp(c)

        a_ps = ps_const.tile([P, N], BF16, name="a_ps")
        b_ps = ps_const.tile([P, N], BF16, name="b_ps")
        a_sb = keep.tile([P, CW], BF16, name="a_sb")
        b_sb = keep.tile([P, CW], BF16, name="b_sb")

        def spread_ab():
            for half in range(2):
                cols = slice(512 * half, 512 * (half + 1))
                nc.tensor.matmul(out=a_ps[:, cols], lhsT=pick_a[:], rhs=ab_row[:, 512 * half : 512 * (half + 1)], start=True, stop=True)
            for half in range(2):
                cols = slice(512 * half, 512 * (half + 1))
                nc.tensor.matmul(out=b_ps[:, cols], lhsT=pick_b[:], rhs=ab_row[:, 512 * half : 512 * (half + 1)], start=True, stop=True)

        def copy_ab():
            if CW > 0:
                nc.scalar.copy(out=a_sb[:, 0:CW], in_=a_ps[:, N - CW : N])
                nc.scalar.copy(out=b_sb[:, 0:CW], in_=b_ps[:, N - CW : N])

        w_g = keep.tile([P, 4 * N], BF16, name="w_g", align_bytes=64)
        w_c = keep.tile([P, N], U32, name="w_c", align_bytes=64)
        w_s = keep.tile([P, N], U8, name="w_s", align_bytes=64)

        def w_interleave(eng_copy, c):
            eng_copy(
                out=w_g[:, 1024 * c : 1024 * (c + 1)].rearrange("p (w j) -> p w j", j=4),
                in_=w_raw[c][:].rearrange("p j w -> p w j"),
            )

        def w_quant(c):
            nc.vector.quantize_mx(
                out=w_c[:, 256 * c : 256 * (c + 1)].bitcast(FP8X4),
                scales=w_s[:, 256 * c : 256 * (c + 1)],
                in_=w_g[:, 1024 * c : 1024 * (c + 1)],
            )

        xs_t = {}
        xt_t = {}
        g_t = {}
        xc_t = {}
        acc_t = {}
        z_t = {}
        sv_t = {}
        neg_t = {}
        t_t = {}
        og_t = {}
        o_t = {}
        o8_t = {}

        def share(j):
            return CW if j < NT - 2 else CW_LAST if j == NT - 2 else 0

        def out_rows(dram, j):
            c, i = divmod(j, 2)
            return dram[256 * c : 256 * (c + 1), :].rearrange("(p i) n -> p i n", i=2)[:, i, :]

        def stage_r(j):
            c, i = divmod(j, 2)
            if c >= 2:
                xs_t[j] = x_split[c][:, 2 * i : 2 * i + 2, :].rearrange("p g x -> p (g x)")
                return
            xs = work.tile([P, 1024], BF16, name="xs")
            xw = x_raw[c][:].bitcast(F32).rearrange("p h (i f q u) -> p i f u h q", i=2, f=2, u=2)
            copy = nc.vector.tensor_copy if j < 2 else nc.scalar.copy
            copy(out=xs[:].bitcast(F32).rearrange("p (f u h q) -> p f u h q", f=2, u=2, h=H), in_=xw[:, i])
            xs_t[j] = xs[:]

        def stage_t_first():
            xw = xs_t[0].bitcast(F32)
            for f in range(2):
                xt = ps_t.tile([P, 2, P], F32, name="xt")
                for u in range(2):
                    b = 2 * f + u
                    nc.tensor.transpose(xt[:, u, :], xw[:, P * b : P * (b + 1)], ident[:])
                xt_t[0, f] = xt
            g_t[0] = work.tile([P, 1024], BF16, name="g", align_bytes=64)
            xc_t[0] = (work.tile([P, 256], U32, name="xc", align_bytes=64), work.tile([P, 256], U8, name="xsc", align_bytes=64))

        def stage_e_first(f):
            nc.scalar.copy(
                out=g_t[0][:, 512 * f : 512 * (f + 1)].bitcast(F32).rearrange("p (r u) -> p r u", u=2),
                in_=xt_t[0, f][:].rearrange("p u r -> p r u"),
            )

        def stage_q_first(f):
            xc, xsc = xc_t[0]
            nc.vector.quantize_mx(
                out=xc[:, P * f : P * (f + 1)].bitcast(FP8X4), scales=xsc[:, P * f : P * (f + 1)], in_=g_t[0][:, 512 * f : 512 * (f + 1)]
            )

        def stage_t(j):
            pool, name = (ps_acc, "acc1") if j == 1 else (ps_t, "xt")
            xt = pool.tile([P, 4, P], F32, name=name)
            xw = xs_t[j].bitcast(F32)
            for f in range(2):
                for u in range(2):
                    b = 2 * f + u
                    words = xw[:, P * b : P * (b + 1)] if j < 4 else xw[:, 256 * f + u : 256 * (f + 1) : 2]
                    nc.tensor.transpose(xt[:, b, :], words, ident[:])
            xt_t[j] = xt

        def stage_e(j):
            g = work.tile([P, 1024], BF16, name="g", align_bytes=64)
            nc.scalar.copy(
                out=g[:].bitcast(F32).rearrange("p (f r u) -> p f r u", f=2, u=2),
                in_=xt_t[j][:].rearrange("p (f u) r -> p f r u", u=2),
            )
            g_t[j] = g

        def stage_q(j):
            xc = work.tile([P, 256], U32, name="xc", align_bytes=64)
            xsc = work.tile([P, 256], U8, name="xsc", align_bytes=64)
            nc.vector.quantize_mx(out=xc[:].bitcast(FP8X4), scales=xsc[:], in_=g_t[j][:])
            xc_t[j] = (xc, xsc)

        def mm(out, xc, xsc, xcols, wcols):
            nc.tensor.matmul_mx(
                out=out,
                lhsT=xc[:, xcols].bitcast(FP8X4),
                lhsT_scale=xsc[:, xcols],
                rhs=w_c[:, wcols].bitcast(FP8X4),
                rhs_scale=w_s[:, wcols],
                start=True,
                stop=True,
            )

        def stage_m(j):
            xc, xsc = xc_t[j]
            acc0 = ps_acc.tile([P, 512], F32, name="acc0")
            acc1 = ps_acc.tile([P, 512], F32, name="acc1")
            mm(acc0[:], xc, xsc, slice(0, 128), slice(0, 512))
            mm(acc1[:, 0:256], xc, xsc, slice(0, 128), slice(512, 768))
            mm(acc1[:, 256:512], xc, xsc, slice(128, 256), slice(768, 1024))
            acc_t[j] = (acc0, acc1)

        def stage_ab(j, b):
            if b == 0:
                z_t[j] = work.tile([P, N], F32, name="z")
                sv_t[j] = stats.tile([P, 8], F32, name="sv")
            nc.vector.scalar_tensor_tensor(
                out=z_t[j][:, 512 * b : 512 * (b + 1)],
                in0=acc_t[j][b][:],
                scalar=1.0,
                in1=inp_sb[j][:, 512 * b : 512 * (b + 1)],
                op0=ALU.mult,
                op1=ALU.add,
                accum_out=sv_t[j][:, b : b + 1],
            )

        def stage_n(j):
            sv = sv_t[j]
            nc.vector.tensor_scalar(
                out=sv[:, 2:3], in0=sv[:, 0:1], scalar1=sv[:, 1:2], scalar2=-1.0 / N, op0=ALU.add, op1=ALU.mult
            )
            neg_t[j] = sv[:, 2:3]

        def stage_n_scalar(j):
            nj = stats.tile([P, 8], F32, name="nj")
            nc.scalar.activation(out=nj[:, 0:2], in_=sv_t[j][:, 0:2], func=ACT.Copy, scale=-1.0 / N, accum_out=nj[:, 2:3])
            neg_t[j] = nj[:, 2:3]

        def stage_p2(j):
            junk = work.tile([P, N], BF16, name="junk")
            nc.scalar.activation(
                out=junk[:],
                in_=z_t[j][:],
                func=ACT.Square,
                bias=neg_t[j],
                scale=1.0,
                accum_out=sq_eps[:, 2 * j : 2 * j + 1],
            )

        def stage_sqrt(j):
            ss = stats.tile([P, 8], F32, name="ss")
            nc.scalar.activation(
                out=ss[:, 0:2],
                in_=sq_eps[:, 2 * j : 2 * j + 2],
                func=ACT.Sqrt,
                scale=1.0 / (N - 1),
                accum_out=sig_eps[:, j : j + 1],
            )

        def stage_p3(j, c0=0, c1=None):
            if c1 is None:
                c1 = N - share(j)
            if c0 == 0:
                t_t[j] = work.tile([P, N], F32, name="t")
            nc.vector.scalar_tensor_tensor(
                out=t_t[j][:, c0:c1], in0=z_t[j][:, c0:c1], scalar=neg_t[j], in1=a_ps[:, c0:c1], op0=ALU.add, op1=ALU.mult
            )

        def stage_rec(j):
            nc.vector.reciprocal(out=sv_t[j][:, 4:5], in_=sig_eps[:, j : j + 1])

        def stage_side(j):
            if share(j) == 0:
                return
            w = share(j)
            u = work.tile([P, CW], F32, name="u")
            nc.gpsimd.tensor_scalar(
                out=u[:, 0:w], in0=z_t[j][:, N - w : N], scalar1=neg_t[j], scalar2=sv_t[j][:, 4:5], op0=ALU.add, op1=ALU.mult
            )
            v = work.tile([P, CW], F32, name="v")
            og = work.tile([P, CW], F32, name="og", bufs=8)
            nc.gpsimd.tensor_tensor(out=v[:, 0:w], in0=u[:, 0:w], in1=a_sb[:, CW - w : CW], op=ALU.mult)
            nc.gpsimd.tensor_tensor(out=og[:, 0:w], in0=v[:, 0:w], in1=b_sb[:, CW - w : CW], op=ALU.add)
            og_t[j] = og

        def stage_p45(j, pieces):
            o = work.tile([P, N], F32, name="o", bufs=8)
            o8 = work.tile([P, N], FP8, name="o8", bufs=8)
            o8_t[j] = o8
            for k in range(len(pieces) - 1):
                cols = slice(pieces[k], pieces[k + 1])
                nc.vector.scalar_tensor_tensor(
                    out=o[:, cols], in0=t_t[j][:, cols], scalar=sv_t[j][:, 4:5], in1=b_ps[:, cols], op0=ALU.mult, op1=ALU.add
                )
                nc.sync.dma_start(out=out_rows(out_0, j)[:, cols], in_=o[:, cols])
            o_t[j] = o

        def stage_last(j, pieces):
            stage_p45(j, pieces)
            o, o8 = o_t[j], o8_t[j]
            stage_bytes(j - 1)
            for k in range(len(pieces) - 1):
                cols = slice(pieces[k], pieces[k + 1])
                if k == 0:
                    nc.scalar.activation(out=o8[:, cols], in_=o[:, cols], func=ACT.Copy, scale=Y_SCALE, saturate=False)
                else:
                    nc.vector.tensor_scalar(
                        out=o8[:, cols], in0=o[:, cols], scalar1=Y_SCALE, scalar2=None, op0=ALU.mult, saturate=False
                    )
                nc.sync.dma_start(out=out_rows(out_1, j)[:, cols], in_=o8[:, cols].bitcast(U8))

        def stage_cast(j):
            c0 = N - share(j)
            nc.scalar.activation(out=o8_t[j][:, 0:c0], in_=o_t[j][:, 0:c0], func=ACT.Copy, scale=Y_SCALE, saturate=False)

        def stage_side_out(j):
            stage_side_store(j)
            stage_side_cast(j)
            stage_bytes(j)

        def stage_side_store(j):
            w = share(j)
            nc.sync.dma_start(out=out_rows(out_0, j)[:, N - w : N], in_=og_t[j][:, 0:w])

        def stage_side_cast(j):
            w = share(j)
            nc.scalar.activation(out=o8_t[j][:, N - w : N], in_=og_t[j][:, 0:w], func=ACT.Copy, scale=Y_SCALE, saturate=False)

        def stage_bytes(j):
            nc.sync.dma_start(out=out_rows(out_1, j), in_=o8_t[j][:].bitcast(U8))

        stage_r(0)
        stage_r(1)
        stage_t_first()
        stage_t(1)
        w_interleave(nc.vector.tensor_copy, 0)
        w_interleave(nc.vector.tensor_copy, 1)
        stage_e_first(0)
        stage_e_first(1)
        w_interleave(nc.scalar.copy, 2)
        w_quant(0)
        w_quant(1)
        w_interleave(nc.vector.tensor_copy, 3)
        stage_q_first(0)
        stage_q_first(1)
        spread_ab()
        stage_e(1)
        w_quant(2)
        w_quant(3)
        stage_m(0)
        stage_r(2)
        stage_t(2)
        copy_ab()

        for k in range(NT - 1):
            stage_ab(k, 0)
            stage_ab(k, 1)
            if k >= 1:
                stage_rec(k - 1)
            stage_q(k + 1)
            stage_m(k + 1)
            if k == 0:
                stage_n(k)
            else:
                stage_n_scalar(k)
            if k >= 2:
                stage_side_out(k - 2)
            stage_p2(k)
            if k >= 1:
                stage_side(k - 1)
                stage_p45(k - 1, [0, N - share(k - 1)])
            stage_p3(k)
            if k + 2 < NT:
                stage_e(k + 2)
            stage_sqrt(k)
            if k + 3 < NT:
                stage_r(k + 3)
                stage_t(k + 3)
            if k >= 1:
                stage_cast(k - 1)
        stage_ab(NT - 1, 0)
        stage_rec(NT - 2)
        stage_ab(NT - 1, 1)
        stage_n(NT - 1)
        stage_side_out(NT - 3)
        stage_p2(NT - 1)
        stage_sqrt(NT - 1)
        stage_side(NT - 2)
        stage_p45(NT - 2, [0, N - share(NT - 2)])
        stage_p3(NT - 1, 0, 768)
        stage_rec(NT - 1)
        stage_p3(NT - 1, 768, N)
        stage_cast(NT - 2)
        stage_side_store(NT - 2)
        stage_side_cast(NT - 2)
        stage_last(NT - 1, [0, 512, 768, N])
